import numpy as np
import ml_dtypes


def mxq(x, axis, fmt="e4m3"):
    dtype, down = {"e4m3": (ml_dtypes.float8_e4m3fn, 7), "e5m2": (ml_dtypes.float8_e5m2, 14)}[fmt]
    v = np.moveaxis(np.asarray(x, np.float32).astype(ml_dtypes.bfloat16).astype(np.float64), axis, -1)
    blocks = v.reshape(v.shape[:-1] + (-1, 32))
    amax = np.abs(blocks).max(-1, keepdims=True)
    byte = np.maximum(np.where(amax > 0, np.frexp(amax)[1] - 1 + 127, 0) - down, 1)
    scale = np.exp2(byte - 127.0)
    codes = (blocks / scale).astype(np.float32).astype(dtype).astype(np.float64)
    return np.moveaxis((codes * scale).reshape(v.shape), -1, axis)


WIDE = False


def mx_kscale(k):
    if not WIDE:
        return np.ones(k)
    levels = np.array([10, -10, 5, -5, 0])
    if k % 512:
        return np.exp2(np.random.permutation(np.resize(levels, k // 32))).repeat(32)
    a = np.empty((k // 512, 16))
    for p in range(k // 512):
        a[p, :8] = np.random.permutation(np.resize(levels, 8))
        for g in range(8):
            far = levels[np.abs(levels - a[p, g]) >= 10]
            a[p, g + 8] = far[np.random.randint(len(far))]
    return np.exp2(a.ravel()).repeat(32)


BF16 = ml_dtypes.bfloat16


def bf(x):
    return np.asarray(x, np.float32).astype(BF16)


def f64(x):
    return np.asarray(x).astype(np.float64)


B, S, D, DV, NS, SD = 4, 1024, 1024, 512, 2, 128
R = B * S


def silu(v):
    return v / (1.0 + np.exp(-v))


def draw0():
    s, r, t = mx_kscale(D), mx_kscale(D), mx_kscale(DV)
    return {"x": bf(np.random.standard_normal((B, S, D)) * r),
            "h": bf(np.random.standard_normal((B, S, D)) * s),
            "Wv": bf(np.random.standard_normal((NS, DV, D)) / np.sqrt(D) * t[:, None] / s),
            "W1": bf(np.random.standard_normal((NS, SD, D + DV)) / np.sqrt(D + DV) / np.concatenate([r, t]))}


def core(x, h, Wv, W1):
    xf = f64(x).reshape(R, D)
    hf = f64(h).reshape(R, D)
    w1 = f64(W1)
    views = mxq(hf, 1, "e4m3") @ mxq(f64(Wv).transpose(0, 2, 1), 1, "e4m3")
    a = mxq(xf, 1, "e4m3") @ mxq(w1[:, :, :D].transpose(0, 2, 1), 1, "e4m3")
    b = mxq(views, 2, "e4m3") @ mxq(w1[:, :, D:].transpose(0, 2, 1), 1, "e4m3")
    return silu(a + b).reshape(NS, B, S, SD)


def e4m3fn_bytes(y):
    return np.clip(np.asarray(y, np.float64), -448.0, 448.0).astype(np.float32).astype(ml_dtypes.float8_e4m3fn).view(np.uint8)


def e4m3fn_values(b):
    return np.asarray(b, np.uint8).view(ml_dtypes.float8_e4m3fn).astype(np.float64)


def setup_inputs():
    d = draw0()
    x0 = np.asarray(d['x']).astype(np.float64)
    s = (np.max(np.abs(x0), axis=(0, 1), keepdims=True) / 448.0).astype(np.float32)
    out = {}
    for k, v in d.items():
        if k == 'x':
            out['x_bytes'] = e4m3fn_bytes(x0 / s.astype(np.float64))
            out['x_scale'] = s
        else:
            out[k] = v
    return out


def reference(x_bytes, x_scale, h, Wv, W1):
    return core(e4m3fn_values(x_bytes) * x_scale.astype(np.float64), h, Wv, W1)

@@ -1,0 +1,319 @@
+from contextlib import ExitStack
+
+import concourse.mybir as mybir
+from concourse.masks import make_identity
+
+FLOPS = 2 * 4096 * 1024 * 1024 + 2 * 4096 * 256 * 1536
+
+F32 = mybir.dt.float32
+BF16 = mybir.dt.bfloat16
+U32 = mybir.dt.uint32
+U8 = mybir.dt.uint8
+F8 = mybir.dt.float8_e4m3fn
+X4 = mybir.dt.float8_e4m3fn_x4
+MULT = mybir.AluOpType.mult
+ACT = mybir.ActivationFunctionType
+
+P = 128
+D = 1024
+ROWS = 4096
+NS = 2
+STEPS = 16
+
+
+def tile_distributedb_pa_t_kernel(tc, x_bytes, x_scale, h, Wv, W1, out):
+    nc = tc.nc
+    x_rows = x_bytes.rearrange("b r k -> (b r) k")
+    h_rows = h.rearrange("b r k -> (b r) k")
+    out_rows = out.rearrange("s b r f -> s (b r) f")
+
+    with ExitStack() as ctx:
+        keep = ctx.enter_context(tc.tile_pool(name="keep", bufs=1))
+        raw = ctx.enter_context(tc.tile_pool(name="raw", bufs=6))
+        wpool = ctx.enter_context(tc.tile_pool(name="wpool", bufs=2))
+        stage = ctx.enter_context(tc.tile_pool(name="stage", bufs=3))
+        psum = ctx.enter_context(tc.psum_pool(name="psum", bufs=2))
+
+        ident = keep.tile([P, P], F32, name="ident", align_bytes=64)
+        make_identity(nc, ident[:])
+        ones = keep.tile([P, 1], F32, name="ones")
+        nc.vector.memset(ones[:], 1.0)
+        warm = keep.tile([P, 1], F32, name="warm")
+        nc.scalar.activation(out=warm[:], in_=ones[:], func=ACT.Silu)
+        scale = keep.tile([P, 8], F32, name="scale")
+        nc.scalar.dma_start(
+            out=scale[:].rearrange("p (g t) -> p g t", g=2),
+            in_=x_scale.rearrange("o b (g p t) -> p (o b g) t", g=2, p=P, t=4),
+        )
+
+        wv_codes = keep.tile([P, 4 * 512], U32, name="wv_codes", align_bytes=256)
+        wv_sc = keep.tile([P, 4 * 512], U8, name="wv_sc", align_bytes=256)
+        w1_codes = keep.tile([P, 6 * P], U32, name="w1_codes", align_bytes=256)
+        w1_sc = keep.tile([P, 6 * P], U8, name="w1_sc", align_bytes=256)
+
+        wv_raw = {}
+        w1_raw = {}
+        h_raw = {}
+        x_raw = {}
+
+        def load_wv(s):
+            src = Wv[s].rearrange("(m t) k -> m t k", t=4)
+            for t in range(4):
+                w = wpool.tile([P, D], BF16, name="wv_raw", bufs=8)
+                nc.sync.dma_start(out=w[:], in_=src[:, t, :])
+                wv_raw[s, t] = w
+
+        def load_w1(s):
+            w = wpool.tile([P, 1536], BF16, name="w1_raw")
+            nc.sync.dma_start(out=w[:], in_=W1[s])
+            w1_raw[s] = w
+
+        def load_h(q, parts):
+            w = raw.tile([P, 4 * D], BF16, name="h_raw")
+            src = h_rows[512 * q : 512 * (q + 1), :].rearrange("(p c) k -> p c k", c=4)
+            h_raw[q] = w
+            return [(w, src, c) for c in parts]
+
+        def load_h_part(item, n):
+            w, src, c = item
+            nc.sync.dma_start(
+                out=w[:, c * D : (c + n) * D].rearrange("p (c k) -> p c k", c=n), in_=src[:, c : c + n, :]
+            )
+
+        def load_x(q):
+            w = raw.tile([P, 4 * D], U8, name="x_raw")
+            src = x_rows[512 * q : 512 * (q + 1), :].rearrange("(p c) k -> p (c k)", c=4)
+            nc.sync.dma_start(out=w[:], in_=src)
+            x_raw[q] = w
+
+        def weight_bank(words, bases):
+            bank = psum.tile([P, 512], F32, name="bank_v", bufs=3)
+            for j, base in enumerate(bases):
+                for u in range(2):
+                    nc.tensor.transpose(
+                        bank[:, (2 * j + u) * P : (2 * j + u + 1) * P], words[:, base + u : base + 256 : 2], ident[:]
+                    )
+            return bank
+
+        def copy_words(on_vector, dst, src):
+            if on_vector:
+                nc.vector.tensor_copy(out=dst, in_=src)
+            else:
+                nc.scalar.copy(out=dst, in_=src)
+
+        wv_stage = {}
+
+        def turn_wv(s, t, on_vector):
+            if t == 0:
+                wv_stage[s] = wpool.tile([P, 2 * 512 * 4], BF16, name="wv_stage", align_bytes=256)
+            bank = weight_bank(wv_raw[s, t][:].bitcast(F32), (0, 256))
+            dst = wv_stage[s][:].bitcast(F32).rearrange("p (g n u) -> p g n u", g=2, u=2)
+            copy_words(
+                on_vector, dst[:, :, t * P : (t + 1) * P, :], bank[:].rearrange("p (g u m) -> p g m u", g=2, u=2)
+            )
+
+        def quant_wv(s, g):
+            c = (2 * s + g) * 512
+            nc.vector.quantize_mx(
+                out=wv_codes[:, c : c + 512].bitcast(X4),
+                scales=wv_sc[:, c : c + 512],
+                in_=wv_stage[s][:, g * 2048 : (g + 1) * 2048],
+            )
+
+        w1_stage = keep.tile([P, 6 * P * 4], BF16, name="w1_stage", align_bytes=256)
+
+        def turn_w1(which, on_vector):
+            dst = w1_stage[:].bitcast(F32).rearrange("p (j f u) -> p j f u", j=6, u=2)
+            bank = psum.tile([P, 512], F32, name="bank_v", bufs=3)
+            parts = ((0, 0), (0, 256)) if which == 0 else ((1, 0), (1, 256)) if which == 1 else ((0, 512), (1, 512))
+            for j, (s, base) in enumerate(parts):
+                words = w1_raw[s][:].bitcast(F32)
+                for u in range(2):
+                    nc.tensor.transpose(
+                        bank[:, (2 * j + u) * P : (2 * j + u + 1) * P], words[:, base + u : base + 256 : 2], ident[:]
+                    )
+            copy_words(
+                on_vector,
+                dst[:, 2 * which : 2 * which + 2, :, :],
+                bank[:].rearrange("p (j u f) -> p j f u", j=2, u=2),
+            )
+
+        def quant_w1():
+            for lo, n in ((0, 4), (4, 2)):
+                nc.vector.quantize_mx(
+                    out=w1_codes[:, lo * P : (lo + n) * P].bitcast(X4),
+                    scales=w1_sc[:, lo * P : (lo + n) * P],
+                    in_=w1_stage[:, lo * 512 : (lo + n) * 512],
+                )
+
+        x_wide = {}
+        x_stage = {}
+        h_stage = {}
+        v_stage = {}
+        xq = {}
+        hq = {}
+        vq = {}
+
+        def widen_x(i):
+            w = stage.tile([P, 2 * D], BF16, name="x_wide", align_bytes=256)
+            src = x_raw[i // 2][:, (i % 2) * 2 * D : (i % 2 + 1) * 2 * D].bitcast(F8)
+            nc.vector.tensor_scalar(
+                out=w[:].rearrange("p (u n e) -> p n u e", u=2, e=2),
+                in0=src.rearrange("p (n u e) -> p n u e", u=2, e=2),
+                scalar1=ones[:, 0:1],
+                scalar2=None,
+                op0=MULT,
+            )
+            x_wide[i] = w
+
+        def turn_x(i):
+            words = x_wide[i][:].bitcast(F32)
+            x_stage[i] = stage.tile([P, 2 * D], BF16, name="x_stage", align_bytes=256)
+            for g in range(2):
+                bank = psum.tile([P, 512], F32, name="bank_x", bufs=2)
+                for u in range(2):
+                    for a in range(2):
+                        c = u * 512 + a * 256 + g * P
+                        nc.tensor.transpose(
+                            bank[:, (2 * u + a) * P : (2 * u + a + 1) * P], words[:, c : c + P], ident[:]
+                        )
+                sc = scale[:, 4 * g : 4 * g + 4].rearrange("p (u e) -> p u e", u=2)
+                nc.vector.tensor_tensor(
+                    out=x_stage[i][:, g * D : (g + 1) * D].rearrange("p (n u e) -> p n u e", u=2, e=2),
+                    in0=bank[:].bitcast(BF16).rearrange("p (u n e) -> p n u e", u=2, e=2),
+                    in1=sc.unsqueeze(1).to_broadcast([P, 256, 2, 2]),
+                    op=MULT,
+                )
+
+        def turn_h(i):
+            words = h_raw[i // 2][:].bitcast(F32)
+            h_stage[i] = stage.tile([P, 2 * D], BF16, name="h_stage", align_bytes=256)
+            for g in range(2):
+                bank = psum.tile([P, 512], F32, name="bank_h", bufs=2)
+                for u in range(2):
+                    for a in range(2):
+                        c = (2 * (i % 2) + a) * 512 + g * 256
+                        nc.tensor.transpose(
+                            bank[:, (2 * u + a) * P : (2 * u + a + 1) * P], words[:, c + u : c + 256 : 2], ident[:]
+                        )
+                nc.scalar.copy(
+                    out=h_stage[i][:].bitcast(F32)[:, g * 512 : (g + 1) * 512].rearrange("p (n u) -> p n u", u=2),
+                    in_=bank[:].rearrange("p (u n) -> p n u", u=2),
+                )
+
+        def quantise(name, src):
+            codes = stage.tile([P, 512], U32, name=name + "_codes", align_bytes=256)
+            scales = stage.tile([P, 512], U8, name=name + "_scales", align_bytes=256)
+            nc.vector.quantize_mx(out=codes[:].bitcast(X4), scales=scales[:], in_=src[:])
+            return codes, scales
+
+        def views(i):
+            codes, scales = hq[i]
+            v_stage[i] = stage.tile([P, 2 * D], BF16, name="v_stage", align_bytes=256)
+            for s in range(NS):
+                for a in range(2):
+                    bank = psum.tile([P, 512], F32, name="bank_v", bufs=3)
+                    for t in range(4):
+                        for g in range(2):
+                            w = (2 * s + g) * 512 + t * P
+                            c = g * 256 + a * P
+                            nc.tensor.matmul_mx(
+                                out=bank[:, t * P : (t + 1) * P],
+                                lhsT=wv_codes[:, w : w + P].bitcast(X4),
+                                lhsT_scale=wv_sc[:, w : w + P],
+                                rhs=codes[:, c : c + P].bitcast(X4),
+                                rhs_scale=scales[:, c : c + P],
+                                start=(g == 0),
+                                stop=(g == 1),
+                            )
+                    k = 2 * s + a
+                    nc.scalar.copy(
+                        out=v_stage[i][:, k * 512 : (k + 1) * 512].rearrange("p (r t) -> p r t", t=4),
+                        in_=bank[:].rearrange("p (t r) -> p r t", t=4),
+                    )
+
+        def finish(i):
+            xc, xs = xq[i]
+            vc, vs = vq[i]
+            bank = psum.tile([P, 512], F32, name="bank_o", bufs=1)
+            for s in range(NS):
+                for a in range(2):
+                    k = 2 * s + a
+                    for j in range(3):
+                        if j < 2:
+                            lhs, lhs_sc, c, w = xc, xs, j * 256 + a * P, (2 * s + j) * P
+                        else:
+                            lhs, lhs_sc, c, w = vc, vs, k * P, (4 + s) * P
+                        nc.tensor.matmul_mx(
+                            out=bank[:, k * P : (k + 1) * P],
+                            lhsT=lhs[:, c : c + P].bitcast(X4),
+                            lhsT_scale=lhs_sc[:, c : c + P],
+                            rhs=w1_codes[:, w : w + P].bitcast(X4),
+                            rhs_scale=w1_sc[:, w : w + P],
+                            start=(j == 0),
+                            stop=(j == 2),
+                        )
+            res = stage.tile([P, 512], F32, name="res", bufs=4)
+            nc.scalar.activation(out=res[:], in_=bank[:], func=ACT.Silu)
+            q, b = i // 2, i % 2
+            dst = out_rows[:, 512 * q : 512 * (q + 1), :].rearrange("s (p c) f -> p s c f", c=4)
+            for s in range(NS):
+                nc.sync.dma_start(
+                    out=dst[:, s, 2 * b : 2 * b + 2, :],
+                    in_=res[:, s * 256 : (s + 1) * 256].rearrange("p (a f) -> p a f", a=2),
+                )
+
+        with tc.manual_schedule():
+            load_wv(0)
+            parts = load_h(0, (0, 2))
+            load_h_part(parts[0], 2)
+            load_x(0)
+            load_wv(1)
+            load_h_part(parts[1], 2)
+            load_w1(0)
+            load_w1(1)
+            for q in (1, 2, 3):
+                load_h_part(load_h(q, (0,))[0], 4)
+                load_x(q)
+
+            for t in range(4):
+                turn_wv(0, t, t % 2 == 0)
+            widen_x(0)
+            turn_x(0)
+            quant_wv(0, 0)
+            quant_wv(0, 1)
+            turn_h(0)
+            for t in range(4):
+                turn_wv(1, t, t % 2 == 0)
+                if t == 1:
+                    hq[0] = quantise("h", h_stage[0])
+            xq[0] = quantise("x", x_stage[0])
+            widen_x(1)
+            turn_w1(0, True)
+            turn_w1(1, False)
+            quant_wv(1, 0)
+            quant_wv(1, 1)
+            turn_w1(2, False)
+
+            for i in range(STEPS):
+                if i > 0:
+                    vq[i - 1] = quantise("v", v_stage[i - 1])
+                if i + 1 < STEPS:
+                    turn_x(i + 1)
+                    turn_h(i + 1)
+                views(i)
+                if i == 0:
+                    quant_w1()
+                if i % 2 == 0 and i // 2 + 4 < STEPS // 2:
+                    q = i // 2 + 4
+                    load_h_part(load_h(q, (0,))[0], 4)
+                    load_x(q)
+                if i > 0:
+                    finish(i - 1)
+                if i + 2 < STEPS:
+                    widen_x(i + 2)
+                if i + 1 < STEPS:
+                    hq[i + 1] = quantise("h", h_stage[i + 1])
+                    xq[i + 1] = quantise("x", x_stage[i + 1])
+            vq[STEPS - 1] = quantise("v", v_stage[STEPS - 1])
+            finish(STEPS - 1)

@@ -16,7 +16,6 @@ ACT = mybir.ActivationFunctionType
 
 P = 128
 D = 1024
-ROWS = 4096
 NS = 2
 STEPS = 16
 
@@ -29,7 +28,7 @@ def tile_distributedb_pa_t_kernel(tc, x_bytes, x_scale, h, Wv, W1, out):
 
     with ExitStack() as ctx:
         keep = ctx.enter_context(tc.tile_pool(name="keep", bufs=1))
-        raw = ctx.enter_context(tc.tile_pool(name="raw", bufs=6))
+        raw = ctx.enter_context(tc.tile_pool(name="raw", bufs=5))
         wpool = ctx.enter_context(tc.tile_pool(name="wpool", bufs=2))
         stage = ctx.enter_context(tc.tile_pool(name="stage", bufs=3))
         psum = ctx.enter_context(tc.psum_pool(name="psum", bufs=2))
@@ -50,50 +49,37 @@ def tile_distributedb_pa_t_kernel(tc, x_bytes, x_scale, h, Wv, W1, out):
         wv_sc = keep.tile([P, 4 * 512], U8, name="wv_sc", align_bytes=256)
         w1_codes = keep.tile([P, 6 * P], U32, name="w1_codes", align_bytes=256)
         w1_sc = keep.tile([P, 6 * P], U8, name="w1_sc", align_bytes=256)
+        w1_stage = keep.tile([P, 6 * P * 4], BF16, name="w1_stage", align_bytes=256)
 
-        wv_raw = {}
-        w1_raw = {}
-        h_raw = {}
-        x_raw = {}
+        wv_raw, w1_raw, h_raw, x_raw = {}, {}, {}, {}
+        wv_stage, h_sorted, x_wide, x_stage, h_stage, v_stage = {}, {}, {}, {}, {}, {}
+        xq, hq, vq, banks = {}, {}, {}, {}
 
-        def load_wv(s):
-            src = Wv[s].rearrange("(m t) k -> m t k", t=4)
-            for t in range(4):
-                w = wpool.tile([P, D], BF16, name="wv_raw", bufs=8)
-                nc.sync.dma_start(out=w[:], in_=src[:, t, :])
-                wv_raw[s, t] = w
+        def load_wv(s, t):
+            w = wpool.tile([P, D], BF16, name="wv_raw", bufs=8)
+            nc.sync.dma_start(out=w[:], in_=Wv[s].rearrange("(m t) k -> m t k", t=4)[:, t, :])
+            wv_raw[s, t] = w
 
         def load_w1(s):
             w = wpool.tile([P, 1536], BF16, name="w1_raw")
             nc.sync.dma_start(out=w[:], in_=W1[s])
             w1_raw[s] = w
 
-        def load_h(q, parts):
-            w = raw.tile([P, 4 * D], BF16, name="h_raw")
-            src = h_rows[512 * q : 512 * (q + 1), :].rearrange("(p c) k -> p c k", c=4)
-            h_raw[q] = w
-            return [(w, src, c) for c in parts]
+        def load_h(i, n=1):
+            q = i // 2
+            if q not in h_raw:
+                h_raw[q] = raw.tile([P, 4 * D], BF16, name="h_raw")
+            src = h_rows[512 * q : 512 * (q + 1), :].rearrange("(p c) k -> p (c k)", c=4)
+            lo, hi = i % 2 * 2 * D, (i % 2 + n) * 2 * D
+            nc.sync.dma_start(out=h_raw[q][:, lo:hi], in_=src[:, lo:hi])
 
-        def load_h_part(item, n):
-            w, src, c = item
-            nc.sync.dma_start(
-                out=w[:, c * D : (c + n) * D].rearrange("p (c k) -> p c k", c=n), in_=src[:, c : c + n, :]
-            )
-
-        def load_x(q):
-            w = raw.tile([P, 4 * D], U8, name="x_raw")
+        def load_x(i, n=1):
+            q = i // 2
+            if q not in x_raw:
+                x_raw[q] = raw.tile([P, 4 * D], U8, name="x_raw")
             src = x_rows[512 * q : 512 * (q + 1), :].rearrange("(p c) k -> p (c k)", c=4)
-            nc.sync.dma_start(out=w[:], in_=src)
-            x_raw[q] = w
-
-        def weight_bank(words, bases):
-            bank = psum.tile([P, 512], F32, name="bank_v", bufs=3)
-            for j, base in enumerate(bases):
-                for u in range(2):
-                    nc.tensor.transpose(
-                        bank[:, (2 * j + u) * P : (2 * j + u + 1) * P], words[:, base + u : base + 256 : 2], ident[:]
-                    )
-            return bank
+            lo, hi = i % 2 * 2 * D, (i % 2 + n) * 2 * D
+            nc.sync.dma_start(out=x_raw[q][:, lo:hi], in_=src[:, lo:hi])
 
         def copy_words(on_vector, dst, src):
             if on_vector:
@@ -101,62 +87,55 @@ def tile_distributedb_pa_t_kernel(tc, x_bytes, x_scale, h, Wv, W1, out):
             else:
                 nc.scalar.copy(out=dst, in_=src)
 
-        wv_stage = {}
-
-        def turn_wv(s, t, on_vector):
-            if t == 0:
-                wv_stage[s] = wpool.tile([P, 2 * 512 * 4], BF16, name="wv_stage", align_bytes=256)
-            bank = weight_bank(wv_raw[s, t][:].bitcast(F32), (0, 256))
-            dst = wv_stage[s][:].bitcast(F32).rearrange("p (g n u) -> p g n u", g=2, u=2)
-            copy_words(
-                on_vector, dst[:, :, t * P : (t + 1) * P, :], bank[:].rearrange("p (g u m) -> p g m u", g=2, u=2)
-            )
-
-        def quant_wv(s, g):
-            c = (2 * s + g) * 512
-            nc.vector.quantize_mx(
-                out=wv_codes[:, c : c + 512].bitcast(X4),
-                scales=wv_sc[:, c : c + 512],
-                in_=wv_stage[s][:, g * 2048 : (g + 1) * 2048],
-            )
-
-        w1_stage = keep.tile([P, 6 * P * 4], BF16, name="w1_stage", align_bytes=256)
-
-        def turn_w1(which, on_vector):
-            dst = w1_stage[:].bitcast(F32).rearrange("p (j f u) -> p j f u", j=6, u=2)
+        def turn_weights(parts):
             bank = psum.tile([P, 512], F32, name="bank_v", bufs=3)
-            parts = ((0, 0), (0, 256)) if which == 0 else ((1, 0), (1, 256)) if which == 1 else ((0, 512), (1, 512))
-            for j, (s, base) in enumerate(parts):
-                words = w1_raw[s][:].bitcast(F32)
+            for j, (words, base) in enumerate(parts):
                 for u in range(2):
-                    nc.tensor.transpose(
-                        bank[:, (2 * j + u) * P : (2 * j + u + 1) * P], words[:, base + u : base + 256 : 2], ident[:]
-                    )
+                    c = 2 * j + u
+                    nc.tensor.transpose(bank[:, c * P : (c + 1) * P], words[:, base + u : base + 256 : 2], ident[:])
+            return bank
+
+        def turn_wv(s, t):
+            words = wv_raw[s, t][:].bitcast(F32)
+            banks["w", s, t] = turn_weights(((words, 0), (words, 256)))
+
+        def copy_wv(s, t, on_vector=False):
+            if t % 2 == 0:
+                wv_stage[s, t // 2] = wpool.tile([P, 2 * D], BF16, name="wv_stage", align_bytes=256, bufs=3)
+            dst = wv_stage[s, t // 2][:, t % 2 * D : (t % 2 + 1) * D].bitcast(F32)
             copy_words(
                 on_vector,
-                dst[:, 2 * which : 2 * which + 2, :, :],
-                bank[:].rearrange("p (j u f) -> p j f u", j=2, u=2),
+                dst.rearrange("p (g m u) -> p g m u", g=2, u=2),
+                banks["w", s, t][:].rearrange("p (g u m) -> p g m u", g=2, u=2),
             )
 
-        def quant_w1():
-            for lo, n in ((0, 4), (4, 2)):
-                nc.vector.quantize_mx(
-                    out=w1_codes[:, lo * P : (lo + n) * P].bitcast(X4),
-                    scales=w1_sc[:, lo * P : (lo + n) * P],
-                    in_=w1_stage[:, lo * 512 : (lo + n) * 512],
-                )
+        def quant_wv(s, half):
+            c = (2 * s + half) * 512
+            nc.vector.quantize_mx(
+                out=wv_codes[:, c : c + 512].bitcast(X4), scales=wv_sc[:, c : c + 512], in_=wv_stage[s, half][:]
+            )
 
-        x_wide = {}
-        x_stage = {}
-        h_stage = {}
-        v_stage = {}
-        xq = {}
-        hq = {}
-        vq = {}
+        def turn_w1(j):
+            banks["1", j] = turn_weights([(w1_raw[s][:].bitcast(F32), 256 * j) for s in range(NS)])
+
+        def copy_w1(j, on_vector=False):
+            dst = w1_stage[:, j * D : (j + 1) * D].bitcast(F32)
+            copy_words(
+                on_vector,
+                dst.rearrange("p (s f u) -> p s f u", s=2, u=2),
+                banks["1", j][:].rearrange("p (s u f) -> p s f u", s=2, u=2),
+            )
+
+        def quant_w1(lo, hi):
+            nc.vector.quantize_mx(
+                out=w1_codes[:, lo * 256 : hi * 256].bitcast(X4),
+                scales=w1_sc[:, lo * 256 : hi * 256],
+                in_=w1_stage[:, lo * D : hi * D],
+            )
 
         def widen_x(i):
             w = stage.tile([P, 2 * D], BF16, name="x_wide", align_bytes=256)
-            src = x_raw[i // 2][:, (i % 2) * 2 * D : (i % 2 + 1) * 2 * D].bitcast(F8)
+            src = x_raw[i // 2][:, i % 2 * 2 * D : (i % 2 + 1) * 2 * D].bitcast(F8)
             nc.vector.tensor_scalar(
                 out=w[:].rearrange("p (u n e) -> p n u e", u=2, e=2),
                 in0=src.rearrange("p (n u e) -> p n u e", u=2, e=2),
@@ -166,154 +145,283 @@ def tile_distributedb_pa_t_kernel(tc, x_bytes, x_scale, h, Wv, W1, out):
             )
             x_wide[i] = w
 
-        def turn_x(i):
+        def turn_x(i, g):
             words = x_wide[i][:].bitcast(F32)
-            x_stage[i] = stage.tile([P, 2 * D], BF16, name="x_stage", align_bytes=256)
-            for g in range(2):
-                bank = psum.tile([P, 512], F32, name="bank_x", bufs=2)
-                for u in range(2):
-                    for a in range(2):
+            bank = psum.tile([P, 512], F32, name="bank_x", bufs=2)
+            for u in range(2):
+                for a in range(2):
+                    c = u * 512 + a * 256 + g * P
+                    k = 2 * u + a
+                    nc.tensor.transpose(bank[:, k * P : (k + 1) * P], words[:, c : c + P], ident[:])
+            banks["x", i, g] = bank
+
+        def scale_x(i, g):
+            if i not in x_stage:
+                x_stage[i] = stage.tile([P, 2 * D], BF16, name="x_stage", align_bytes=256)
+            sc = scale[:, 4 * g : 4 * g + 4].rearrange("p (u e) -> p u e", u=2)
+            nc.vector.tensor_tensor(
+                out=x_stage[i][:, g * D : (g + 1) * D].rearrange("p (n u e) -> p n u e", u=2, e=2),
+                in0=banks["x", i, g][:].bitcast(BF16).rearrange("p (u n e) -> p n u e", u=2, e=2),
+                in1=sc.unsqueeze(1).to_broadcast([P, 256, 2, 2]),
+                op=MULT,
+            )
+
+        def sort_h(i, on_vector=False):
+            w = stage.tile([P, 2 * D], BF16, name="h_sorted", align_bytes=256, bufs=2)
+            src = h_raw[i // 2][:, i % 2 * 2 * D : (i % 2 + 1) * 2 * D].bitcast(F32)
+            copy_words(
+                on_vector,
+                w[:].bitcast(F32).rearrange("p (u n) -> p u n", u=2),
+                src.rearrange("p (n u) -> p u n", u=2),
+            )
+            h_sorted[i] = w
+
+        def turn_h(i, g):
+            bank = psum.tile([P, 512], F32, name="bank_h", bufs=2)
+            for u in range(2):
+                for a in range(2):
+                    if i in h_sorted:
                         c = u * 512 + a * 256 + g * P
-                        nc.tensor.transpose(
-                            bank[:, (2 * u + a) * P : (2 * u + a + 1) * P], words[:, c : c + P], ident[:]
-                        )
-                sc = scale[:, 4 * g : 4 * g + 4].rearrange("p (u e) -> p u e", u=2)
-                nc.vector.tensor_tensor(
-                    out=x_stage[i][:, g * D : (g + 1) * D].rearrange("p (n u e) -> p n u e", u=2, e=2),
-                    in0=bank[:].bitcast(BF16).rearrange("p (u n e) -> p n u e", u=2, e=2),
-                    in1=sc.unsqueeze(1).to_broadcast([P, 256, 2, 2]),
-                    op=MULT,
-                )
-
-        def turn_h(i):
-            words = h_raw[i // 2][:].bitcast(F32)
-            h_stage[i] = stage.tile([P, 2 * D], BF16, name="h_stage", align_bytes=256)
-            for g in range(2):
-                bank = psum.tile([P, 512], F32, name="bank_h", bufs=2)
-                for u in range(2):
-                    for a in range(2):
+                        w = h_sorted[i][:].bitcast(F32)[:, c : c + P]
+                    else:
                         c = (2 * (i % 2) + a) * 512 + g * 256
-                        nc.tensor.transpose(
-                            bank[:, (2 * u + a) * P : (2 * u + a + 1) * P], words[:, c + u : c + 256 : 2], ident[:]
-                        )
-                nc.scalar.copy(
-                    out=h_stage[i][:].bitcast(F32)[:, g * 512 : (g + 1) * 512].rearrange("p (n u) -> p n u", u=2),
-                    in_=bank[:].rearrange("p (u n) -> p n u", u=2),
-                )
+                        w = h_raw[i // 2][:].bitcast(F32)[:, c + u : c + 256 : 2]
+                    k = 2 * u + a
+                    nc.tensor.transpose(bank[:, k * P : (k + 1) * P], w, ident[:])
+            banks["h", i, g] = bank
 
-        def quantise(name, src):
+        def copy_h(i, g, on_vector=False):
+            if i not in h_stage:
+                h_stage[i] = stage.tile([P, 2 * D], BF16, name="h_stage", align_bytes=256)
+            copy_words(
+                on_vector,
+                h_stage[i][:].bitcast(F32)[:, g * 512 : (g + 1) * 512].rearrange("p (n u) -> p n u", u=2),
+                banks["h", i, g][:].rearrange("p (u n) -> p n u", u=2),
+            )
+
+        def quantise(name, src, pieces=1):
             codes = stage.tile([P, 512], U32, name=name + "_codes", align_bytes=256)
             scales = stage.tile([P, 512], U8, name=name + "_scales", align_bytes=256)
-            nc.vector.quantize_mx(out=codes[:].bitcast(X4), scales=scales[:], in_=src[:])
+            n = 512 // pieces
+            for k in range(pieces):
+                nc.vector.quantize_mx(
+                    out=codes[:, k * n : (k + 1) * n].bitcast(X4),
+                    scales=scales[:, k * n : (k + 1) * n],
+                    in_=src[:, 4 * k * n : 4 * (k + 1) * n],
+                )
             return codes, scales
 
-        def views(i):
+        def quant_h(i):
+            hq[i] = quantise("h", h_stage[i])
+
+        def quant_x(i):
+            xq[i] = quantise("x", x_stage[i])
+
+        def quant_v(i, pieces=1):
+            vq[i] = quantise("v", v_stage[i], pieces)
+
+        def views(i, s):
             codes, scales = hq[i]
-            v_stage[i] = stage.tile([P, 2 * D], BF16, name="v_stage", align_bytes=256)
-            for s in range(NS):
-                for a in range(2):
-                    bank = psum.tile([P, 512], F32, name="bank_v", bufs=3)
-                    for t in range(4):
-                        for g in range(2):
-                            w = (2 * s + g) * 512 + t * P
-                            c = g * 256 + a * P
-                            nc.tensor.matmul_mx(
-                                out=bank[:, t * P : (t + 1) * P],
-                                lhsT=wv_codes[:, w : w + P].bitcast(X4),
-                                lhsT_scale=wv_sc[:, w : w + P],
-                                rhs=codes[:, c : c + P].bitcast(X4),
-                                rhs_scale=scales[:, c : c + P],
-                                start=(g == 0),
-                                stop=(g == 1),
-                            )
-                    k = 2 * s + a
-                    nc.scalar.copy(
-                        out=v_stage[i][:, k * 512 : (k + 1) * 512].rearrange("p (r t) -> p r t", t=4),
-                        in_=bank[:].rearrange("p (t r) -> p r t", t=4),
-                    )
+            if i not in v_stage:
+                v_stage[i] = stage.tile([P, 2 * D], BF16, name="v_stage", align_bytes=256)
+            for a in range(2):
+                bank = psum.tile([P, 512], F32, name="bank_v", bufs=3)
+                for t in range(4):
+                    for g in range(2):
+                        w = ((4 * s + t) * 2 + g) * P
+                        c = g * 256 + a * P
+                        nc.tensor.matmul_mx(
+                            out=bank[:, t * P : (t + 1) * P],
+                            lhsT=wv_codes[:, w : w + P].bitcast(X4),
+                            lhsT_scale=wv_sc[:, w : w + P],
+                            rhs=codes[:, c : c + P].bitcast(X4),
+                            rhs_scale=scales[:, c : c + P],
+                            start=(g == 0),
+                            stop=(g == 1),
+                        )
+                k = 2 * s + a
+                nc.scalar.copy(
+                    out=v_stage[i][:, k * 512 : (k + 1) * 512].rearrange("p (r t) -> p r t", t=4),
+                    in_=bank[:].rearrange("p (t r) -> p r t", t=4),
+                )
 
         def finish(i):
             xc, xs = xq[i]
             vc, vs = vq[i]
             bank = psum.tile([P, 512], F32, name="bank_o", bufs=1)
-            for s in range(NS):
-                for a in range(2):
-                    k = 2 * s + a
-                    for j in range(3):
-                        if j < 2:
-                            lhs, lhs_sc, c, w = xc, xs, j * 256 + a * P, (2 * s + j) * P
-                        else:
-                            lhs, lhs_sc, c, w = vc, vs, k * P, (4 + s) * P
-                        nc.tensor.matmul_mx(
-                            out=bank[:, k * P : (k + 1) * P],
-                            lhsT=lhs[:, c : c + P].bitcast(X4),
-                            lhsT_scale=lhs_sc[:, c : c + P],
-                            rhs=w1_codes[:, w : w + P].bitcast(X4),
-                            rhs_scale=w1_sc[:, w : w + P],
-                            start=(j == 0),
-                            stop=(j == 2),
-                        )
+            for a in range(2):
+                for j in range(2):
+                    c = j * 256 + a * P
+                    nc.tensor.matmul_mx(
+                        out=bank[:, a * 256 : (a + 1) * 256],
+                        lhsT=xc[:, c : c + P].bitcast(X4),
+                        lhsT_scale=xs[:, c : c + P],
+                        rhs=w1_codes[:, j * 256 : (j + 1) * 256].bitcast(X4),
+                        rhs_scale=w1_sc[:, j * 256 : (j + 1) * 256],
+                        start=(j == 0),
+                        stop=False,
+                    )
+                for s in range(NS):
+                    c = (2 * s + a) * P
+                    w = (4 + s) * P
+                    k = 2 * a + s
+                    nc.tensor.matmul_mx(
+                        out=bank[:, k * P : (k + 1) * P],
+                        lhsT=vc[:, c : c + P].bitcast(X4),
+                        lhsT_scale=vs[:, c : c + P],
+                        rhs=w1_codes[:, w : w + P].bitcast(X4),
+                        rhs_scale=w1_sc[:, w : w + P],
+                        start=False,
+                        stop=(s == 1),
+                    )
             res = stage.tile([P, 512], F32, name="res", bufs=4)
-            nc.scalar.activation(out=res[:], in_=bank[:], func=ACT.Silu)
-            q, b = i // 2, i % 2
-            dst = out_rows[:, 512 * q : 512 * (q + 1), :].rearrange("s (p c) f -> p s c f", c=4)
+            nc.scalar.activation(
+                out=res[:].rearrange("p (s a f) -> p s a f", s=2, a=2),
+                in_=bank[:].rearrange("p (a s f) -> p s a f", s=2, a=2),
+                func=ACT.Silu,
+            )
+            dst = out_rows[:, 512 * (i // 2) : 512 * (i // 2 + 1), :].rearrange("s (p c) f -> p s c f", c=4)
+            c = i % 2 * 2
             for s in range(NS):
                 nc.sync.dma_start(
-                    out=dst[:, s, 2 * b : 2 * b + 2, :],
+                    out=dst[:, s, c : c + 2, :],
                     in_=res[:, s * 256 : (s + 1) * 256].rearrange("p (a f) -> p a f", a=2),
                 )
 
+        def x_part_apart(i):
+            xc, xs = xq[i]
+            for k in range(4):
+                s, a = divmod(k, 2)
+                bank = psum.tile([P, 512], F32, name="bank_x" if k < 2 else "bank_h", bufs=2)
+                for j in range(2):
+                    c = j * 256 + a * P
+                    w = (2 * j + s) * P
+                    nc.tensor.matmul_mx(
+                        out=bank[:, 0:P],
+                        lhsT=xc[:, c : c + P].bitcast(X4),
+                        lhsT_scale=xs[:, c : c + P],
+                        rhs=w1_codes[:, w : w + P].bitcast(X4),
+                        rhs_scale=w1_sc[:, w : w + P],
+                        start=(j == 0),
+                        stop=False,
+                    )
+                banks["o", k] = bank
+
+        def finish_apart(i, pieces=1):
+            vc, vs = vq[i]
+            dst = out_rows[:, 512 * (i // 2) : 512 * (i // 2 + 1), :].rearrange("s (p c) f -> p s c f", c=4)
+            for k in range(4):
+                s, a = divmod(k, 2)
+                w = (4 + s) * P
+                nc.tensor.matmul_mx(
+                    out=banks["o", k][:, 0:P],
+                    lhsT=vc[:, k * P : (k + 1) * P].bitcast(X4),
+                    lhsT_scale=vs[:, k * P : (k + 1) * P],
+                    rhs=w1_codes[:, w : w + P].bitcast(X4),
+                    rhs_scale=w1_sc[:, w : w + P],
+                    start=False,
+                    stop=True,
+                )
+                res = stage.tile([P, P], F32, name="res_apart", bufs=4)
+                nc.scalar.activation(out=res[:], in_=banks["o", k][:, 0:P], func=ACT.Silu)
+                nc.sync.dma_start(out=dst[:, s, i % 2 * 2 + a, :], in_=res[:])
+
         with tc.manual_schedule():
-            load_wv(0)
-            parts = load_h(0, (0, 2))
-            load_h_part(parts[0], 2)
+            load_h(0)
             load_x(0)
-            load_wv(1)
-            load_h_part(parts[1], 2)
+            load_wv(0, 0)
+            load_wv(0, 1)
+            load_wv(0, 2)
+            load_wv(0, 3)
+            load_x(1)
+            load_wv(1, 0)
+            load_wv(1, 1)
+            load_wv(1, 2)
+            load_wv(1, 3)
+            load_h(1)
             load_w1(0)
             load_w1(1)
-            for q in (1, 2, 3):
-                load_h_part(load_h(q, (0,))[0], 4)
-                load_x(q)
-
-            for t in range(4):
-                turn_wv(0, t, t % 2 == 0)
+            load_h(2, 2)
+            load_x(2, 2)
+            load_h(4, 2)
+            load_x(4, 2)
+            load_h(6, 2)
+            load_x(6, 2)
             widen_x(0)
-            turn_x(0)
+            turn_h(0, 0)
+            copy_h(0, 0)
+            turn_h(0, 1)
+            copy_h(0, 1)
+            turn_x(0, 0)
+            scale_x(0, 0)
+            turn_x(0, 1)
+            scale_x(0, 1)
+            turn_wv(0, 0)
+            copy_wv(0, 0)
+            turn_wv(0, 1)
+            copy_wv(0, 1)
+            turn_wv(0, 2)
+            copy_wv(0, 2)
+            turn_wv(0, 3)
+            copy_wv(0, 3)
+            quant_h(0)
             quant_wv(0, 0)
+            quant_x(0)
             quant_wv(0, 1)
-            turn_h(0)
-            for t in range(4):
-                turn_wv(1, t, t % 2 == 0)
-                if t == 1:
-                    hq[0] = quantise("h", h_stage[0])
-            xq[0] = quantise("x", x_stage[0])
             widen_x(1)
-            turn_w1(0, True)
-            turn_w1(1, False)
+            turn_wv(1, 0)
+            copy_wv(1, 0)
+            turn_wv(1, 1)
+            copy_wv(1, 1)
+            views(0, 0)
+            turn_wv(1, 2)
+            copy_wv(1, 2)
+            turn_wv(1, 3)
+            copy_wv(1, 3)
             quant_wv(1, 0)
+            turn_x(1, 0)
+            scale_x(1, 0)
+            turn_x(1, 1)
+            scale_x(1, 1)
             quant_wv(1, 1)
-            turn_w1(2, False)
-
-            for i in range(STEPS):
-                if i > 0:
-                    vq[i - 1] = quantise("v", v_stage[i - 1])
+            turn_h(1, 0)
+            copy_h(1, 0)
+            turn_h(1, 1)
+            copy_h(1, 1)
+            turn_w1(0)
+            copy_w1(0)
+            turn_w1(1)
+            copy_w1(1)
+            turn_w1(2)
+            copy_w1(2)
+            views(0, 1)
+            quant_h(1)
+            widen_x(2)
+            quant_x(1)
+            quant_w1(0, 2)
+            quant_w1(2, 3)
+            for i in range(1, STEPS):
+                quant_v(i - 1)
                 if i + 1 < STEPS:
-                    turn_x(i + 1)
-                    turn_h(i + 1)
-                views(i)
-                if i == 0:
-                    quant_w1()
-                if i % 2 == 0 and i // 2 + 4 < STEPS // 2:
-                    q = i // 2 + 4
-                    load_h_part(load_h(q, (0,))[0], 4)
-                    load_x(q)
-                if i > 0:
-                    finish(i - 1)
+                    for g in range(2):
+                        turn_x(i + 1, g)
+                        scale_x(i + 1, g)
+                    for g in range(2):
+                        turn_h(i + 1, g)
+                        copy_h(i + 1, g)
+                views(i, 0)
+                views(i, 1)
+                if i % 2 == 0 and i + 6 < STEPS:
+                    load_h(i + 6, 2)
+                    load_x(i + 6, 2)
+                finish(i - 1)
                 if i + 2 < STEPS:
                     widen_x(i + 2)
                 if i + 1 < STEPS:
-                    hq[i + 1] = quantise("h", h_stage[i + 1])
-                    xq[i + 1] = quantise("x", x_stage[i + 1])
-            vq[STEPS - 1] = quantise("v", v_stage[STEPS - 1])
-            finish(STEPS - 1)
+                    quant_h(i + 1)
+                    quant_x(i + 1)
+                if i + 3 < STEPS:
+                    sort_h(i + 3)
+            x_part_apart(STEPS - 1)
+            quant_v(STEPS - 1, 4)
+            finish_apart(STEPS - 1)

@@ -18,6 +18,9 @@ P = 128
 D = 1024
 NS = 2
 STEPS = 16
+APART = ()
+SORT_V = ()
+SORT_S = ()
 
 
 def tile_distributedb_pa_t_kernel(tc, x_bytes, x_scale, h, Wv, W1, out):
@@ -52,8 +55,9 @@ def tile_distributedb_pa_t_kernel(tc, x_bytes, x_scale, h, Wv, W1, out):
         w1_stage = keep.tile([P, 6 * P * 4], BF16, name="w1_stage", align_bytes=256)
 
         wv_raw, w1_raw, h_raw, x_raw = {}, {}, {}, {}
-        wv_stage, h_sorted, x_wide, x_stage, h_stage, v_stage = {}, {}, {}, {}, {}, {}
-        xq, hq, vq, banks = {}, {}, {}, {}
+        wv_stage, h_sorted, x_wide, hx_stage, v_stage = {}, {}, {}, {}, {}
+        hxq, vq, banks = {}, {}, {}
+        scale_rows = keep.tile([P, D], F32, name="scale_rows")
 
         def load_wv(s, t):
             w = wpool.tile([P, D], BF16, name="wv_raw", bufs=8)
@@ -80,6 +84,11 @@ def tile_distributedb_pa_t_kernel(tc, x_bytes, x_scale, h, Wv, W1, out):
             src = x_rows[512 * q : 512 * (q + 1), :].rearrange("(p c) k -> p (c k)", c=4)
             lo, hi = i % 2 * 2 * D, (i % 2 + n) * 2 * D
             nc.sync.dma_start(out=x_raw[q][:, lo:hi], in_=src[:, lo:hi])
+
+        def prefetch(i):
+            if i % 2 == 0 and i + 6 < STEPS:
+                load_h(i + 6, 2)
+                load_x(i + 6, 2)
 
         def copy_words(on_vector, dst, src):
             if on_vector:
@@ -133,8 +142,22 @@ def tile_distributedb_pa_t_kernel(tc, x_bytes, x_scale, h, Wv, W1, out):
                 in_=w1_stage[:, lo * D : hi * D],
             )
 
+        def load_scale_rows():
+            nc.sync.dma_start(out=scale_rows[:], in_=x_scale.rearrange("o b k -> (o b k)").partition_broadcast(P))
+
         def widen_x(i):
             w = stage.tile([P, 2 * D], BF16, name="x_wide", align_bytes=256)
+            x_wide[i] = w
+            if i in APART:
+                for a in range(2):
+                    c = (2 * (i % 2) + a) * D
+                    nc.vector.tensor_tensor(
+                        out=w[:, a * D : (a + 1) * D],
+                        in0=x_raw[i // 2][:, c : c + D].bitcast(F8),
+                        in1=scale_rows[:],
+                        op=MULT,
+                    )
+                return
             src = x_raw[i // 2][:, i % 2 * 2 * D : (i % 2 + 1) * 2 * D].bitcast(F8)
             nc.vector.tensor_scalar(
                 out=w[:].rearrange("p (u n e) -> p n u e", u=2, e=2),
@@ -143,30 +166,52 @@ def tile_distributedb_pa_t_kernel(tc, x_bytes, x_scale, h, Wv, W1, out):
                 scalar2=None,
                 op0=MULT,
             )
-            x_wide[i] = w
 
         def turn_x(i, g):
             words = x_wide[i][:].bitcast(F32)
             bank = psum.tile([P, 512], F32, name="bank_x", bufs=2)
             for u in range(2):
                 for a in range(2):
-                    c = u * 512 + a * 256 + g * P
+                    if i in APART:
+                        c = a * 512 + g * 256
+                        w = words[:, c + u : c + 256 : 2]
+                    else:
+                        c = u * 512 + a * 256 + g * P
+                        w = words[:, c : c + P]
                     k = 2 * u + a
-                    nc.tensor.transpose(bank[:, k * P : (k + 1) * P], words[:, c : c + P], ident[:])
+                    nc.tensor.transpose(bank[:, k * P : (k + 1) * P], w, ident[:])
             banks["x", i, g] = bank
 
-        def scale_x(i, g):
-            if i not in x_stage:
-                x_stage[i] = stage.tile([P, 2 * D], BF16, name="x_stage", align_bytes=256)
+        def stage_of(kind, i):
+            j = i - 1 if kind == "h" else i
+            if j not in hx_stage:
+                hx_stage[j] = stage.tile([P, 4 * D], BF16, name="hx_stage", align_bytes=256)
+            return hx_stage[j]
+
+        def unload(i, kind, g, on_vector):
+            c = (g if kind == "h" else 2 + g) * D
+            copy_words(
+                on_vector,
+                stage_of(kind, i)[:, c : c + D].bitcast(F32).rearrange("p (n u) -> p n u", u=2),
+                banks[kind, i, g][:].rearrange("p (u n) -> p n u", u=2),
+            )
+
+        def scale_x(i, g, on_vector=False):
+            if i in APART:
+                unload(i, "x", g, on_vector)
+                return
             sc = scale[:, 4 * g : 4 * g + 4].rearrange("p (u e) -> p u e", u=2)
             nc.vector.tensor_tensor(
-                out=x_stage[i][:, g * D : (g + 1) * D].rearrange("p (n u e) -> p n u e", u=2, e=2),
+                out=stage_of("x", i)[:, (2 + g) * D : (3 + g) * D].rearrange("p (n u e) -> p n u e", u=2, e=2),
                 in0=banks["x", i, g][:].bitcast(BF16).rearrange("p (u n e) -> p n u e", u=2, e=2),
                 in1=sc.unsqueeze(1).to_broadcast([P, 256, 2, 2]),
                 op=MULT,
             )
 
-        def sort_h(i, on_vector=False):
+        def sort_h(i):
+            on_vector = i in SORT_V
+            if not on_vector and i not in SORT_S:
+                return
             w = stage.tile([P, 2 * D], BF16, name="h_sorted", align_bytes=256, bufs=2)
             src = h_raw[i // 2][:, i % 2 * 2 * D : (i % 2 + 1) * 2 * D].bitcast(F32)
             copy_words(
@@ -191,18 +236,13 @@ def tile_distributedb_pa_t_kernel(tc, x_bytes, x_scale, h, Wv, W1, out):
             banks["h", i, g] = bank
 
         def copy_h(i, g, on_vector=False):
-            if i not in h_stage:
-                h_stage[i] = stage.tile([P, 2 * D], BF16, name="h_stage", align_bytes=256)
-            copy_words(
-                on_vector,
-                h_stage[i][:].bitcast(F32)[:, g * 512 : (g + 1) * 512].rearrange("p (n u) -> p n u", u=2),
-                banks["h", i, g][:].rearrange("p (u n) -> p n u", u=2),
-            )
+            unload(i, "h", g, on_vector)
 
         def quantise(name, src, pieces=1):
-            codes = stage.tile([P, 512], U32, name=name + "_codes", align_bytes=256)
-            scales = stage.tile([P, 512], U8, name=name + "_scales", align_bytes=256)
-            n = 512 // pieces
+            n = src.shape[1] // 4
+            codes = stage.tile([P, n], U32, name=name + "_codes", align_bytes=256)
+            scales = stage.tile([P, n], U8, name=name + "_scales", align_bytes=256)
+            n = n // pieces
             for k in range(pieces):
                 nc.vector.quantize_mx(
                     out=codes[:, k * n : (k + 1) * n].bitcast(X4),
@@ -211,17 +251,25 @@ def tile_distributedb_pa_t_kernel(tc, x_bytes, x_scale, h, Wv, W1, out):
                 )
             return codes, scales
 
-        def quant_h(i):
-            hq[i] = quantise("h", h_stage[i])
-
-        def quant_x(i):
-            xq[i] = quantise("x", x_stage[i])
+        def quant_hx(i, kinds="hx"):
+            if i == STEPS - 1:
+                kinds = "x"
+            if i not in hxq:
+                hxq[i] = (
+                    stage.tile([P, 1024], U32, name="hx_codes", align_bytes=256),
+                    stage.tile([P, 1024], U8, name="hx_scales", align_bytes=256),
+                )
+            codes, scales = hxq[i]
+            lo, hi = (0 if "h" in kinds else 512), (1024 if "x" in kinds else 512)
+            nc.vector.quantize_mx(
+                out=codes[:, lo:hi].bitcast(X4), scales=scales[:, lo:hi], in_=hx_stage[i][:, 4 * lo : 4 * hi]
+            )
 
         def quant_v(i, pieces=1):
             vq[i] = quantise("v", v_stage[i], pieces)
 
         def views(i, s):
-            codes, scales = hq[i]
+            codes, scales = hxq[i - 1]
             if i not in v_stage:
                 v_stage[i] = stage.tile([P, 2 * D], BF16, name="v_stage", align_bytes=256)
             for a in range(2):
@@ -246,12 +294,12 @@ def tile_distributedb_pa_t_kernel(tc, x_bytes, x_scale, h, Wv, W1, out):
                 )
 
         def finish(i):
-            xc, xs = xq[i]
+            xc, xs = hxq[i]
             vc, vs = vq[i]
             bank = psum.tile([P, 512], F32, name="bank_o", bufs=1)
             for a in range(2):
                 for j in range(2):
-                    c = j * 256 + a * P
+                    c = 512 + j * 256 + a * P
                     nc.tensor.matmul_mx(
                         out=bank[:, a * 256 : (a + 1) * 256],
                         lhsT=xc[:, c : c + P].bitcast(X4),
@@ -289,12 +337,12 @@ def tile_distributedb_pa_t_kernel(tc, x_bytes, x_scale, h, Wv, W1, out):
                 )
 
         def x_part_apart(i):
-            xc, xs = xq[i]
+            xc, xs = hxq[i]
             for k in range(4):
                 s, a = divmod(k, 2)
                 bank = psum.tile([P, 512], F32, name="bank_x" if k < 2 else "bank_h", bufs=2)
                 for j in range(2):
-                    c = j * 256 + a * P
+                    c = 512 + j * 256 + a * P
                     w = (2 * j + s) * P
                     nc.tensor.matmul_mx(
                         out=bank[:, 0:P],
@@ -329,99 +377,86 @@ def tile_distributedb_pa_t_kernel(tc, x_bytes, x_scale, h, Wv, W1, out):
         with tc.manual_schedule():
             load_h(0)
             load_x(0)
-            load_wv(0, 0)
             load_wv(0, 1)
             load_wv(0, 2)
-            load_wv(0, 3)
-            load_x(1)
+            load_wv(0, 0)
             load_wv(1, 0)
-            load_wv(1, 1)
+            load_wv(0, 3)
             load_wv(1, 2)
-            load_wv(1, 3)
-            load_h(1)
-            load_w1(0)
-            load_w1(1)
-            load_h(2, 2)
-            load_x(2, 2)
-            load_h(4, 2)
-            load_x(4, 2)
-            load_h(6, 2)
-            load_x(6, 2)
-            widen_x(0)
-            turn_h(0, 0)
-            copy_h(0, 0)
+            load_wv(1, 1)
             turn_h(0, 1)
+            load_h(1)
+            widen_x(0)
+            load_x(1)
+            load_wv(1, 3)
+            turn_h(0, 0)
+            turn_wv(0, 1)
+            load_w1(0)
+            load_x(2, 2)
+            load_w1(1)
             copy_h(0, 1)
+            copy_h(0, 0, True)
             turn_x(0, 0)
-            scale_x(0, 0)
-            turn_x(0, 1)
-            scale_x(0, 1)
             turn_wv(0, 0)
             copy_wv(0, 0)
-            turn_wv(0, 1)
-            copy_wv(0, 1)
             turn_wv(0, 2)
             copy_wv(0, 2)
+            copy_wv(0, 1, True)
             turn_wv(0, 3)
-            copy_wv(0, 3)
-            quant_h(0)
-            quant_wv(0, 0)
-            quant_x(0)
-            quant_wv(0, 1)
-            widen_x(1)
             turn_wv(1, 0)
-            copy_wv(1, 0)
             turn_wv(1, 1)
-            copy_wv(1, 1)
-            views(0, 0)
+            load_h(2, 2)
+            scale_x(0, 0)
+            quant_wv(0, 0)
+            copy_wv(0, 3)
+            quant_wv(0, 1)
+            quant_hx(-1, "h")
+            turn_x(0, 1)
+            copy_wv(1, 0)
             turn_wv(1, 2)
-            copy_wv(1, 2)
-            turn_wv(1, 3)
-            copy_wv(1, 3)
-            quant_wv(1, 0)
-            turn_x(1, 0)
-            scale_x(1, 0)
-            turn_x(1, 1)
-            scale_x(1, 1)
-            quant_wv(1, 1)
+            load_x(6, 2)
+            copy_wv(1, 2, True)
             turn_h(1, 0)
-            copy_h(1, 0)
+            turn_wv(1, 3)
+            load_x(4, 2)
+            copy_wv(1, 1)
             turn_h(1, 1)
+            copy_h(1, 0)
+            scale_x(0, 1)
+            load_h(4, 2)
+            copy_wv(1, 3)
+            quant_wv(1, 1)
             copy_h(1, 1)
+            views(0, 0)
+            widen_x(1)
             turn_w1(0)
             copy_w1(0)
+            load_h(6, 2)
             turn_w1(1)
+            quant_wv(1, 0)
+            quant_hx(0)
             copy_w1(1)
+            quant_w1(0, 2)
             turn_w1(2)
             copy_w1(2)
-            views(0, 1)
-            quant_h(1)
-            widen_x(2)
-            quant_x(1)
-            quant_w1(0, 2)
             quant_w1(2, 3)
+            views(0, 1)
             for i in range(1, STEPS):
+                prefetch(i)
+                turn_x(i, 1)
                 quant_v(i - 1)
-                if i + 1 < STEPS:
-                    for g in range(2):
-                        turn_x(i + 1, g)
-                        scale_x(i + 1, g)
-                    for g in range(2):
-                        turn_h(i + 1, g)
-                        copy_h(i + 1, g)
+                turn_x(i, 0)
+                if i + 1 < STEPS: turn_h(i + 1, 0)
+                if i + 1 < STEPS: copy_h(i + 1, 0)
+                if i + 1 < STEPS: turn_h(i + 1, 1)
+                scale_x(i, 0)
+                scale_x(i, 1)
+                if i + 1 < STEPS: copy_h(i + 1, 1)
+                if i + 1 < STEPS: widen_x(i + 1)
                 views(i, 0)
                 views(i, 1)
-                if i % 2 == 0 and i + 6 < STEPS:
-                    load_h(i + 6, 2)
-                    load_x(i + 6, 2)
+                quant_hx(i)
                 finish(i - 1)
-                if i + 2 < STEPS:
-                    widen_x(i + 2)
-                if i + 1 < STEPS:
-                    quant_h(i + 1)
-                    quant_x(i + 1)
-                if i + 3 < STEPS:
-                    sort_h(i + 3)
             x_part_apart(STEPS - 1)
             quant_v(STEPS - 1, 4)
             finish_apart(STEPS - 1)

from contextlib import ExitStack

import concourse.mybir as mybir
from concourse.masks import make_identity

FLOPS = 2 * 4096 * 1024 * 1024 + 2 * 4096 * 256 * 1536

F32 = mybir.dt.float32
BF16 = mybir.dt.bfloat16
U32 = mybir.dt.uint32
U8 = mybir.dt.uint8
F8 = mybir.dt.float8_e4m3fn
X4 = mybir.dt.float8_e4m3fn_x4
MULT = mybir.AluOpType.mult
ACT = mybir.ActivationFunctionType

P = 128
D = 1024
NS = 2
STEPS = 16
APART = ()
SORT_V = ()
SORT_S = ()


def tile_distributedb_pa_t_kernel(tc, x_bytes, x_scale, h, Wv, W1, out):
    nc = tc.nc
    x_rows = x_bytes.rearrange("b r k -> (b r) k")
    h_rows = h.rearrange("b r k -> (b r) k")
    out_rows = out.rearrange("s b r f -> s (b r) f")

    with ExitStack() as ctx:
        keep = ctx.enter_context(tc.tile_pool(name="keep", bufs=1))
        raw = ctx.enter_context(tc.tile_pool(name="raw", bufs=5))
        wpool = ctx.enter_context(tc.tile_pool(name="wpool", bufs=2))
        stage = ctx.enter_context(tc.tile_pool(name="stage", bufs=3))
        psum = ctx.enter_context(tc.psum_pool(name="psum", bufs=2))

        ident = keep.tile([P, P], F32, name="ident", align_bytes=64)
        make_identity(nc, ident[:])
        ones = keep.tile([P, 1], F32, name="ones")
        nc.vector.memset(ones[:], 1.0)
        warm = keep.tile([P, 1], F32, name="warm")
        nc.scalar.activation(out=warm[:], in_=ones[:], func=ACT.Silu)
        scale = keep.tile([P, 8], F32, name="scale")
        nc.scalar.dma_start(
            out=scale[:].rearrange("p (g t) -> p g t", g=2),
            in_=x_scale.rearrange("o b (g p t) -> p (o b g) t", g=2, p=P, t=4),
        )

        wv_codes = keep.tile([P, 4 * 512], U32, name="wv_codes", align_bytes=256)
        wv_sc = keep.tile([P, 4 * 512], U8, name="wv_sc", align_bytes=256)
        w1_codes = keep.tile([P, 6 * P], U32, name="w1_codes", align_bytes=256)
        w1_sc = keep.tile([P, 6 * P], U8, name="w1_sc", align_bytes=256)
        w1_stage = keep.tile([P, 6 * P * 4], BF16, name="w1_stage", align_bytes=256)

        wv_raw, w1_raw, h_raw, x_raw = {}, {}, {}, {}
        wv_stage, h_sorted, x_wide, hx_stage, v_stage = {}, {}, {}, {}, {}
        hxq, vq, banks = {}, {}, {}
        scale_rows = keep.tile([P, D], F32, name="scale_rows")

        def load_wv(s, t):
            w = wpool.tile([P, D], BF16, name="wv_raw", bufs=8)
            nc.sync.dma_start(out=w[:], in_=Wv[s].rearrange("(m t) k -> m t k", t=4)[:, t, :])
            wv_raw[s, t] = w

        def load_w1(s):
            w = wpool.tile([P, 1536], BF16, name="w1_raw")
            nc.sync.dma_start(out=w[:], in_=W1[s])
            w1_raw[s] = w

        def load_h(i, n=1):
            q = i // 2
            if q not in h_raw:
                h_raw[q] = raw.tile([P, 4 * D], BF16, name="h_raw")
            src = h_rows[512 * q : 512 * (q + 1), :].rearrange("(p c) k -> p (c k)", c=4)
            lo, hi = i % 2 * 2 * D, (i % 2 + n) * 2 * D
            nc.sync.dma_start(out=h_raw[q][:, lo:hi], in_=src[:, lo:hi])

        def load_x(i, n=1):
            q = i // 2
            if q not in x_raw:
                x_raw[q] = raw.tile([P, 4 * D], U8, name="x_raw")
            src = x_rows[512 * q : 512 * (q + 1), :].rearrange("(p c) k -> p (c k)", c=4)
            lo, hi = i % 2 * 2 * D, (i % 2 + n) * 2 * D
            nc.sync.dma_start(out=x_raw[q][:, lo:hi], in_=src[:, lo:hi])

        def prefetch(i):
            if i % 2 == 0 and i + 6 < STEPS:
                load_h(i + 6, 2)
                load_x(i + 6, 2)

        def copy_words(on_vector, dst, src):
            if on_vector:
                nc.vector.tensor_copy(out=dst, in_=src)
            else:
                nc.scalar.copy(out=dst, in_=src)

        def turn_weights(parts):
            bank = psum.tile([P, 512], F32, name="bank_v", bufs=3)
            for j, (words, base) in enumerate(parts):
                for u in range(2):
                    c = 2 * j + u
                    nc.tensor.transpose(bank[:, c * P : (c + 1) * P], words[:, base + u : base + 256 : 2], ident[:])
            return bank

        def turn_wv(s, t):
            words = wv_raw[s, t][:].bitcast(F32)
            banks["w", s, t] = turn_weights(((words, 0), (words, 256)))

        def copy_wv(s, t, on_vector=False):
            if t % 2 == 0:
                wv_stage[s, t // 2] = wpool.tile([P, 2 * D], BF16, name="wv_stage", align_bytes=256, bufs=3)
            dst = wv_stage[s, t // 2][:, t % 2 * D : (t % 2 + 1) * D].bitcast(F32)
            copy_words(
                on_vector,
                dst.rearrange("p (g m u) -> p g m u", g=2, u=2),
                banks["w", s, t][:].rearrange("p (g u m) -> p g m u", g=2, u=2),
            )

        def quant_wv(s, half):
            c = (2 * s + half) * 512
            nc.vector.quantize_mx(
                out=wv_codes[:, c : c + 512].bitcast(X4), scales=wv_sc[:, c : c + 512], in_=wv_stage[s, half][:]
            )

        def turn_w1(j):
            banks["1", j] = turn_weights([(w1_raw[s][:].bitcast(F32), 256 * j) for s in range(NS)])

        def copy_w1(j, on_vector=False):
            dst = w1_stage[:, j * D : (j + 1) * D].bitcast(F32)
            copy_words(
                on_vector,
                dst.rearrange("p (s f u) -> p s f u", s=2, u=2),
                banks["1", j][:].rearrange("p (s u f) -> p s f u", s=2, u=2),
            )

        def quant_w1(lo, hi):
            nc.vector.quantize_mx(
                out=w1_codes[:, lo * 256 : hi * 256].bitcast(X4),
                scales=w1_sc[:, lo * 256 : hi * 256],
                in_=w1_stage[:, lo * D : hi * D],
            )

        def load_scale_rows():
            nc.sync.dma_start(out=scale_rows[:], in_=x_scale.rearrange("o b k -> (o b k)").partition_broadcast(P))

        def widen_x(i):
            w = stage.tile([P, 2 * D], BF16, name="x_wide", align_bytes=256)
            x_wide[i] = w
            if i in APART:
                for a in range(2):
                    c = (2 * (i % 2) + a) * D
                    nc.vector.tensor_tensor(
                        out=w[:, a * D : (a + 1) * D],
                        in0=x_raw[i // 2][:, c : c + D].bitcast(F8),
                        in1=scale_rows[:],
                        op=MULT,
                    )
                return
            src = x_raw[i // 2][:, i % 2 * 2 * D : (i % 2 + 1) * 2 * D].bitcast(F8)
            nc.vector.tensor_scalar(
                out=w[:].rearrange("p (u n e) -> p n u e", u=2, e=2),
                in0=src.rearrange("p (n u e) -> p n u e", u=2, e=2),
                scalar1=ones[:, 0:1],
                scalar2=None,
                op0=MULT,
            )

        def turn_x(i, g):
            words = x_wide[i][:].bitcast(F32)
            bank = psum.tile([P, 512], F32, name="bank_x", bufs=2)
            for u in range(2):
                for a in range(2):
                    if i in APART:
                        c = a * 512 + g * 256
                        w = words[:, c + u : c + 256 : 2]
                    else:
                        c = u * 512 + a * 256 + g * P
                        w = words[:, c : c + P]
                    k = 2 * u + a
                    nc.tensor.transpose(bank[:, k * P : (k + 1) * P], w, ident[:])
            banks["x", i, g] = bank

        def stage_of(kind, i):
            j = i - 1 if kind == "h" else i
            if j not in hx_stage:
                hx_stage[j] = stage.tile([P, 4 * D], BF16, name="hx_stage", align_bytes=256)
            return hx_stage[j]

        def unload(i, kind, g, on_vector):
            c = (g if kind == "h" else 2 + g) * D
            copy_words(
                on_vector,
                stage_of(kind, i)[:, c : c + D].bitcast(F32).rearrange("p (n u) -> p n u", u=2),
                banks[kind, i, g][:].rearrange("p (u n) -> p n u", u=2),
            )

        def scale_x(i, g, on_vector=False):
            if i in APART:
                unload(i, "x", g, on_vector)
                return
            sc = scale[:, 4 * g : 4 * g + 4].rearrange("p (u e) -> p u e", u=2)
            nc.vector.tensor_tensor(
                out=stage_of("x", i)[:, (2 + g) * D : (3 + g) * D].rearrange("p (n u e) -> p n u e", u=2, e=2),
                in0=banks["x", i, g][:].bitcast(BF16).rearrange("p (u n e) -> p n u e", u=2, e=2),
                in1=sc.unsqueeze(1).to_broadcast([P, 256, 2, 2]),
                op=MULT,
            )

        def sort_h(i):
            on_vector = i in SORT_V
            if not on_vector and i not in SORT_S:
                return
            w = stage.tile([P, 2 * D], BF16, name="h_sorted", align_bytes=256, bufs=2)
            src = h_raw[i // 2][:, i % 2 * 2 * D : (i % 2 + 1) * 2 * D].bitcast(F32)
            copy_words(
                on_vector,
                w[:].bitcast(F32).rearrange("p (u n) -> p u n", u=2),
                src.rearrange("p (n u) -> p u n", u=2),
            )
            h_sorted[i] = w

        def turn_h(i, g):
            bank = psum.tile([P, 512], F32, name="bank_h", bufs=2)
            for u in range(2):
                for a in range(2):
                    if i in h_sorted:
                        c = u * 512 + a * 256 + g * P
                        w = h_sorted[i][:].bitcast(F32)[:, c : c + P]
                    else:
                        c = (2 * (i % 2) + a) * 512 + g * 256
                        w = h_raw[i // 2][:].bitcast(F32)[:, c + u : c + 256 : 2]
                    k = 2 * u + a
                    nc.tensor.transpose(bank[:, k * P : (k + 1) * P], w, ident[:])
            banks["h", i, g] = bank

        def copy_h(i, g, on_vector=False):
            unload(i, "h", g, on_vector)

        def quantise(name, src, pieces=1):
            n = src.shape[1] // 4
            codes = stage.tile([P, n], U32, name=name + "_codes", align_bytes=256)
            scales = stage.tile([P, n], U8, name=name + "_scales", align_bytes=256)
            n = n // pieces
            for k in range(pieces):
                nc.vector.quantize_mx(
                    out=codes[:, k * n : (k + 1) * n].bitcast(X4),
                    scales=scales[:, k * n : (k + 1) * n],
                    in_=src[:, 4 * k * n : 4 * (k + 1) * n],
                )
            return codes, scales

        def quant_hx(i, kinds="hx"):
            if i == STEPS - 1:
                kinds = "x"
            if i not in hxq:
                hxq[i] = (
                    stage.tile([P, 1024], U32, name="hx_codes", align_bytes=256),
                    stage.tile([P, 1024], U8, name="hx_scales", align_bytes=256),
                )
            codes, scales = hxq[i]
            lo, hi = (0 if "h" in kinds else 512), (1024 if "x" in kinds else 512)
            nc.vector.quantize_mx(
                out=codes[:, lo:hi].bitcast(X4), scales=scales[:, lo:hi], in_=hx_stage[i][:, 4 * lo : 4 * hi]
            )

        def quant_v(i, pieces=1):
            vq[i] = quantise("v", v_stage[i], pieces)

        def views(i, s):
            codes, scales = hxq[i - 1]
            if i not in v_stage:
                v_stage[i] = stage.tile([P, 2 * D], BF16, name="v_stage", align_bytes=256)
            for a in range(2):
                bank = psum.tile([P, 512], F32, name="bank_v", bufs=3)
                for t in range(4):
                    for g in range(2):
                        w = ((4 * s + t) * 2 + g) * P
                        c = g * 256 + a * P
                        nc.tensor.matmul_mx(
                            out=bank[:, t * P : (t + 1) * P],
                            lhsT=wv_codes[:, w : w + P].bitcast(X4),
                            lhsT_scale=wv_sc[:, w : w + P],
                            rhs=codes[:, c : c + P].bitcast(X4),
                            rhs_scale=scales[:, c : c + P],
                            start=(g == 0),
                            stop=(g == 1),
                        )
                k = 2 * s + a
                nc.scalar.copy(
                    out=v_stage[i][:, k * 512 : (k + 1) * 512].rearrange("p (r t) -> p r t", t=4),
                    in_=bank[:].rearrange("p (t r) -> p r t", t=4),
                )

        def finish(i):
            xc, xs = hxq[i]
            vc, vs = vq[i]
            bank = psum.tile([P, 512], F32, name="bank_o", bufs=1)
            for a in range(2):
                for j in range(2):
                    c = 512 + j * 256 + a * P
                    nc.tensor.matmul_mx(
                        out=bank[:, a * 256 : (a + 1) * 256],
                        lhsT=xc[:, c : c + P].bitcast(X4),
                        lhsT_scale=xs[:, c : c + P],
                        rhs=w1_codes[:, j * 256 : (j + 1) * 256].bitcast(X4),
                        rhs_scale=w1_sc[:, j * 256 : (j + 1) * 256],
                        start=(j == 0),
                        stop=False,
                    )
                for s in range(NS):
                    c = (2 * s + a) * P
                    w = (4 + s) * P
                    k = 2 * a + s
                    nc.tensor.matmul_mx(
                        out=bank[:, k * P : (k + 1) * P],
                        lhsT=vc[:, c : c + P].bitcast(X4),
                        lhsT_scale=vs[:, c : c + P],
                        rhs=w1_codes[:, w : w + P].bitcast(X4),
                        rhs_scale=w1_sc[:, w : w + P],
                        start=False,
                        stop=(s == 1),
                    )
            res = stage.tile([P, 512], F32, name="res", bufs=4)
            nc.scalar.activation(
                out=res[:].rearrange("p (s a f) -> p s a f", s=2, a=2),
                in_=bank[:].rearrange("p (a s f) -> p s a f", s=2, a=2),
                func=ACT.Silu,
            )
            dst = out_rows[:, 512 * (i // 2) : 512 * (i // 2 + 1), :].rearrange("s (p c) f -> p s c f", c=4)
            c = i % 2 * 2
            for s in range(NS):
                nc.sync.dma_start(
                    out=dst[:, s, c : c + 2, :],
                    in_=res[:, s * 256 : (s + 1) * 256].rearrange("p (a f) -> p a f", a=2),
                )

        def x_part_apart(i):
            xc, xs = hxq[i]
            for k in range(4):
                s, a = divmod(k, 2)
                bank = psum.tile([P, 512], F32, name="bank_x" if k < 2 else "bank_h", bufs=2)
                for j in range(2):
                    c = 512 + j * 256 + a * P
                    w = (2 * j + s) * P
                    nc.tensor.matmul_mx(
                        out=bank[:, 0:P],
                        lhsT=xc[:, c : c + P].bitcast(X4),
                        lhsT_scale=xs[:, c : c + P],
                        rhs=w1_codes[:, w : w + P].bitcast(X4),
                        rhs_scale=w1_sc[:, w : w + P],
                        start=(j == 0),
                        stop=False,
                    )
                banks["o", k] = bank

        def finish_apart(i, pieces=1):
            vc, vs = vq[i]
            dst = out_rows[:, 512 * (i // 2) : 512 * (i // 2 + 1), :].rearrange("s (p c) f -> p s c f", c=4)
            for k in range(4):
                s, a = divmod(k, 2)
                w = (4 + s) * P
                nc.tensor.matmul_mx(
                    out=banks["o", k][:, 0:P],
                    lhsT=vc[:, k * P : (k + 1) * P].bitcast(X4),
                    lhsT_scale=vs[:, k * P : (k + 1) * P],
                    rhs=w1_codes[:, w : w + P].bitcast(X4),
                    rhs_scale=w1_sc[:, w : w + P],
                    start=False,
                    stop=True,
                )
                res = stage.tile([P, P], F32, name="res_apart", bufs=4)
                nc.scalar.activation(out=res[:], in_=banks["o", k][:, 0:P], func=ACT.Silu)
                nc.sync.dma_start(out=dst[:, s, i % 2 * 2 + a, :], in_=res[:])

        with tc.manual_schedule():
            load_h(0)
            load_x(0)
            load_wv(0, 1)
            load_wv(0, 2)
            load_wv(0, 0)
            load_wv(1, 0)
            load_wv(0, 3)
            load_wv(1, 2)
            load_wv(1, 1)
            turn_h(0, 1)
            load_h(1)
            widen_x(0)
            load_x(1)
            load_wv(1, 3)
            turn_h(0, 0)
            turn_wv(0, 1)
            load_w1(0)
            load_x(2, 2)
            load_w1(1)
            copy_h(0, 1)
            copy_h(0, 0, True)
            turn_x(0, 0)
            turn_wv(0, 0)
            copy_wv(0, 0)
            turn_wv(0, 2)
            copy_wv(0, 2)
            copy_wv(0, 1, True)
            turn_wv(0, 3)
            turn_wv(1, 0)
            turn_wv(1, 1)
            load_h(2, 2)
            scale_x(0, 0)
            quant_wv(0, 0)
            copy_wv(0, 3)
            quant_wv(0, 1)
            quant_hx(-1, "h")
            turn_x(0, 1)
            copy_wv(1, 0)
            turn_wv(1, 2)
            load_x(6, 2)
            copy_wv(1, 2, True)
            turn_h(1, 0)
            turn_wv(1, 3)
            load_x(4, 2)
            copy_wv(1, 1)
            turn_h(1, 1)
            copy_h(1, 0)
            scale_x(0, 1)
            load_h(4, 2)
            copy_wv(1, 3)
            quant_wv(1, 1)
            copy_h(1, 1)
            views(0, 0)
            widen_x(1)
            turn_w1(0)
            copy_w1(0)
            load_h(6, 2)
            turn_w1(1)
            quant_wv(1, 0)
            quant_hx(0)
            copy_w1(1)
            quant_w1(0, 2)
            turn_w1(2)
            copy_w1(2)
            quant_w1(2, 3)
            views(0, 1)
            for i in range(1, STEPS):
                prefetch(i)
                turn_x(i, 1)
                quant_v(i - 1)
                turn_x(i, 0)
                if i + 1 < STEPS: turn_h(i + 1, 0)
                if i + 1 < STEPS: copy_h(i + 1, 0)
                if i + 1 < STEPS: turn_h(i + 1, 1)
                scale_x(i, 0)
                scale_x(i, 1)
                if i + 1 < STEPS: copy_h(i + 1, 1)
                if i + 1 < STEPS: widen_x(i + 1)
                views(i, 0)
                views(i, 1)
                quant_hx(i)
                finish(i - 1)
            x_part_apart(STEPS - 1)
            quant_v(STEPS - 1, 4)
            finish_apart(STEPS - 1)
